import numpy as np
import ml_dtypes


def mxq(x, axis, fmt="e4m3"):
    dtype, down = {"e4m3": (ml_dtypes.float8_e4m3fn, 7), "e5m2": (ml_dtypes.float8_e5m2, 14)}[fmt]
    v = np.moveaxis(np.asarray(x, np.float32).astype(ml_dtypes.bfloat16).astype(np.float64), axis, -1)
    blocks = v.reshape(v.shape[:-1] + (-1, 32))
    amax = np.abs(blocks).max(-1, keepdims=True)
    byte = np.maximum(np.where(amax > 0, np.frexp(amax)[1] - 1 + 127, 0) - down, 1)
    scale = np.exp2(byte - 127.0)
    codes = (blocks / scale).astype(np.float32).astype(dtype).astype(np.float64)
    return np.moveaxis((codes * scale).reshape(v.shape), -1, axis)


WIDE = False


def mx_kscale(k):
    if not WIDE:
        return np.ones(k)
    levels = np.array([10, -10, 5, -5, 0])
    if k % 512:
        return np.exp2(np.random.permutation(np.resize(levels, k // 32))).repeat(32)
    a = np.empty((k // 512, 16))
    for p in range(k // 512):
        a[p, :8] = np.random.permutation(np.resize(levels, 8))
        for g in range(8):
            far = levels[np.abs(levels - a[p, g]) >= 10]
            a[p, g + 8] = far[np.random.randint(len(far))]
    return np.exp2(a.ravel()).repeat(32)


BF16 = ml_dtypes.bfloat16


def bf(x):
    return np.asarray(x, np.float32).astype(BF16)


def f64(x):
    return np.asarray(x).astype(np.float64)


B, S, HID, H, D = 4, 2048, 512, 2, 64
QKV = 3 * H * D


def rotate_half(x):
    x1, x2 = x[..., : x.shape[-1] // 2], x[..., x.shape[-1] // 2 :]
    return np.concatenate((-x2, x1), axis=-1)


def setup_inputs():
    s = mx_kscale(HID)
    return {"hidden_states": bf(np.random.standard_normal((B, S, HID)) * s),
            "cos": bf(np.random.uniform(size=(S, D))),
            "sin": bf(np.random.uniform(size=(S, D))),
            "w_qkv": bf(np.random.standard_normal((HID, QKV)) * 2.0 / np.sqrt(HID) / s[:, None])}


def reference(hidden_states, cos, sin, w_qkv):
    qkv = mxq(f64(hidden_states), 2, "e4m3") @ mxq(f64(w_qkv), 0, "e4m3")
    qkv = qkv.reshape(B, S, 3 * H, D)
    q, k, v = qkv[:, :, :H], qkv[:, :, H:2 * H], qkv[:, :, 2 * H:]
    c = f64(cos)[:, None, :]
    sn = f64(sin)[:, None, :]
    q_rot = q * c + rotate_half(q) * sn
    k_rot = k * c + rotate_half(k) * sn
    return q_rot, k_rot, v

@@ -1,0 +1,259 @@
+from contextlib import ExitStack
+
+import concourse.mybir as mybir
+from concourse.masks import make_identity
+
+F32 = mybir.dt.float32
+BF16 = mybir.dt.bfloat16
+U32 = mybir.dt.uint32
+U8 = mybir.dt.uint8
+FP8X4 = mybir.dt.float8_e4m3fn_x4
+MULT = mybir.AluOpType.mult
+ADD = mybir.AluOpType.add
+
+P = 128
+BATCH = 4
+SEQ = 2048
+HID = 512
+HEAD = 64
+HALF = 32
+QK_COLS = 256
+V_COLS = 128
+T_PER_PART = SEQ // P
+TILES = 4
+GROUPS_PER_BATCH = T_PER_PART // TILES
+N_GROUPS = BATCH * GROUPS_PER_BATCH
+
+FLOPS = 2 * BATCH * SEQ * HID * (QK_COLS + V_COLS)
+
+
+def tile_attention_pa_t_kernel(tc, hidden_states, cos, sin, w_qkv, out_0, out_1, out_2):
+    nc = tc.nc
+    xv = hidden_states.rearrange("b (p t) k -> b p t k", t=T_PER_PART)
+    qv = out_0.rearrange("b (p t) h d -> b p t (h d)", t=T_PER_PART)
+    kv = out_1.rearrange("b (p t) h d -> b p t (h d)", t=T_PER_PART)
+    vv = out_2.rearrange("b (p t) h d -> b p t (h d)", t=T_PER_PART)
+
+    with ExitStack() as ctx:
+        const = ctx.enter_context(tc.tile_pool(name="const", bufs=1))
+        xpool = ctx.enter_context(tc.tile_pool(name="xpool", bufs=N_GROUPS))
+        gpool = ctx.enter_context(tc.tile_pool(name="gpool", bufs=3))
+        cpool = ctx.enter_context(tc.tile_pool(name="cpool", bufs=3))
+        rpool = ctx.enter_context(tc.tile_pool(name="rpool", bufs=3))
+        opool = ctx.enter_context(tc.tile_pool(name="opool", bufs=N_GROUPS))
+        ps_x = ctx.enter_context(tc.psum_pool(name="ps_x", bufs=2))
+        ps_qk = ctx.enter_context(tc.psum_pool(name="ps_qk", bufs=4))
+        ps_v = ctx.enter_context(tc.psum_pool(name="ps_v", bufs=2))
+        ctx.enter_context(tc.manual_schedule())
+
+        x_tiles = {}
+        xt_tiles = {}
+        grouped_tiles = {}
+        code_tiles = {}
+        qk_banks = {}
+        v_banks = {}
+        prod_tiles = {}
+        out_tiles = {}
+
+        ident = const.tile([P, P], F32, name="ident")
+        make_identity(nc, ident[:])
+
+        w_raw = const.tile([P, 4 * (QK_COLS + V_COLS)], BF16, name="w_raw")
+        w_grp = const.tile([P, 4 * (QK_COLS + V_COLS)], BF16, name="w_grp", align_bytes=64)
+        w_codes = const.tile([P, QK_COLS + V_COLS], U32, name="w_codes", align_bytes=64)
+        w_scales = const.tile([P, QK_COLS + V_COLS], U8, name="w_scales", align_bytes=64)
+        cos_sb = const.tile([P, T_PER_PART * HEAD], BF16, name="cos_sb")
+        sin_sb = const.tile([P, T_PER_PART * HEAD], BF16, name="sin_sb")
+        cos_v = cos_sb[:].rearrange("p (t d) -> p t d", d=HEAD)
+        sin_v = sin_sb[:].rearrange("p (t d) -> p t d", d=HEAD)
+
+        def load_x(i):
+            b, gg = divmod(i, GROUPS_PER_BATCH)
+            x_sb = xpool.tile([P, TILES * HID], BF16, name="x_sb", tag="x_sb")
+            nc.sync.dma_start(
+                out=x_sb[:].rearrange("p (t k) -> p t k", k=HID),
+                in_=xv[b, :, gg * TILES : (gg + 1) * TILES, :],
+            )
+            x_tiles[i] = x_sb
+
+        def transpose_group(i):
+            words = x_tiles[i][:].bitcast(F32)
+            banks = []
+            for pr in range(2):
+                xt = ps_x.tile([P, 512], F32, name="xt", tag="xt")
+                for j in range(2):
+                    for u in range(2):
+                        base = (2 * pr + j) * 256
+                        nc.tensor.transpose(
+                            xt[:, u * 256 + j * P : u * 256 + (j + 1) * P],
+                            words[:, base + u : base + 256 : 2],
+                            ident[:],
+                        )
+                banks.append(xt)
+            xt_tiles[i] = banks
+
+        def copy_group(i):
+            grouped = gpool.tile([P, TILES * HID], BF16, name="grouped", tag="grouped", align_bytes=64)
+            gw = grouped[:].bitcast(F32)
+            for pr in range(2):
+                nc.scalar.copy(
+                    out=gw[:, pr * 512 : (pr + 1) * 512].rearrange("p (m u) -> p m u", u=2),
+                    in_=xt_tiles[i][pr][:].rearrange("p (u m) -> p m u", u=2),
+                )
+            grouped_tiles[i] = grouped
+
+        def quantise_group(i):
+            codes = cpool.tile([P, TILES * P], U32, name="codes", tag="codes", align_bytes=64)
+            scales = cpool.tile([P, TILES * P], U8, name="scales", tag="scales", align_bytes=64)
+            nc.vector.quantize_mx(
+                out=codes[:].bitcast(FP8X4), scales=scales[:], in_=grouped_tiles[i][:]
+            )
+            code_tiles[i] = (codes, scales)
+
+        def project_group(i):
+            codes, scales = code_tiles[i]
+            v_ps = ps_v.tile([P, 512], F32, name="v_ps", tag="v_ps")
+            banks = []
+            for pr in range(2):
+                qk_ps = ps_qk.tile([P, 512], F32, name="qk_ps", tag="qk_ps")
+                for j in range(2):
+                    tl = 2 * pr + j
+                    cols = slice(tl * P, (tl + 1) * P)
+                    nc.tensor.matmul_mx(
+                        out=qk_ps[:, j * QK_COLS : (j + 1) * QK_COLS],
+                        lhsT=codes[:, cols].bitcast(FP8X4),
+                        lhsT_scale=scales[:, cols],
+                        rhs=w_codes[:, 0:QK_COLS].bitcast(FP8X4),
+                        rhs_scale=w_scales[:, 0:QK_COLS],
+                        start=True,
+                        stop=True,
+                    )
+                    nc.tensor.matmul_mx(
+                        out=v_ps[:, cols],
+                        lhsT=codes[:, cols].bitcast(FP8X4),
+                        lhsT_scale=scales[:, cols],
+                        rhs=w_codes[:, QK_COLS : QK_COLS + V_COLS].bitcast(FP8X4),
+                        rhs_scale=w_scales[:, QK_COLS : QK_COLS + V_COLS],
+                        start=True,
+                        stop=True,
+                    )
+                banks.append(qk_ps)
+            qk_banks[i] = banks
+            v_banks[i] = v_ps
+
+        def rope_products(i, pr):
+            gg = i % GROUPS_PER_BATCH
+            if pr == 0:
+                pa = rpool.tile([P, TILES * QK_COLS], F32, name="pa", tag="pa")
+                pb = rpool.tile([P, TILES * QK_COLS], F32, name="pb", tag="pb")
+                prod_tiles[i] = (pa, pb)
+            pa, pb = prod_tiles[i]
+            t0 = gg * TILES + 2 * pr
+            bank = qk_banks[i][pr][:].rearrange("p (j h d) -> p j h d", j=2, d=HEAD)
+            pa_v = pa[:].rearrange("p (t h d) -> p t h d", t=TILES, d=HEAD)[:, 2 * pr : 2 * pr + 2, :, :]
+            pb_v = pb[:].rearrange("p (t h d) -> p t h d", t=TILES, d=HEAD)[:, 2 * pr : 2 * pr + 2, :, :]
+            nc.vector.tensor_tensor(
+                out=pa_v,
+                in0=bank,
+                in1=cos_v[:, t0 : t0 + 2, :].unsqueeze(2).to_broadcast([P, 2, 4, HEAD]),
+                op=MULT,
+            )
+            nc.vector.tensor_tensor(
+                out=pb_v[:, :, :, 0:HALF],
+                in0=bank[:, :, :, HALF:HEAD],
+                in1=sin_v[:, t0 : t0 + 2, 0:HALF].unsqueeze(2).to_broadcast([P, 2, 4, HALF]),
+                op=MULT,
+            )
+            nc.vector.tensor_tensor(
+                out=pb_v[:, :, :, HALF:HEAD],
+                in0=bank[:, :, :, 0:HALF],
+                in1=sin_v[:, t0 : t0 + 2, HALF:HEAD].unsqueeze(2).to_broadcast([P, 2, 4, HALF]),
+                op=MULT,
+            )
+
+        def rope_sum(i, engine, t_lo, t_hi):
+            pa, pb = prod_tiles[i]
+            if i not in out_tiles:
+                qk_out = opool.tile([P, 2 * TILES * P], F32, name="qk_out", tag="qk_out")
+                out_tiles[i] = qk_out
+            qk_out = out_tiles[i]
+            engine.tensor_tensor(
+                out=qk_out[:].rearrange("p (g t c) -> p t g c", g=2, c=P)[:, t_lo:t_hi, :, :],
+                in0=pa[:].rearrange("p (t g c) -> p t g c", g=2, c=P)[:, t_lo:t_hi, :, :],
+                in1=pb[:].rearrange("p (t g c) -> p t g c", g=2, c=P)[:, t_lo:t_hi, :, :],
+                op=ADD,
+            )
+
+        def copy_v(i):
+            v_out = opool.tile([P, TILES * P], F32, name="v_out", tag="v_out")
+            nc.scalar.copy(out=v_out[:], in_=v_banks[i][:])
+            return v_out
+
+        def store_group(i, v_out):
+            b, gg = divmod(i, GROUPS_PER_BATCH)
+            ts = slice(gg * TILES, (gg + 1) * TILES)
+            qk_out = out_tiles[i]
+            nc.sync.dma_start(out=vv[b, :, ts, :], in_=v_out[:].rearrange("p (t c) -> p t c", c=P))
+            nc.sync.dma_start(
+                out=qv[b, :, ts, :], in_=qk_out[:, 0 : TILES * P].rearrange("p (t c) -> p t c", c=P)
+            )
+            nc.sync.dma_start(
+                out=kv[b, :, ts, :],
+                in_=qk_out[:, TILES * P : 2 * TILES * P].rearrange("p (t c) -> p t c", c=P),
+            )
+
+        load_x(0)
+        nc.sync.dma_start(
+            out=w_raw[:],
+            in_=w_qkv.rearrange("(q t) c -> q (t c)", t=4),
+        )
+        load_x(1)
+        nc.sync.dma_start(out=cos_v, in_=cos.rearrange("(p t) d -> p t d", t=T_PER_PART))
+        nc.sync.dma_start(out=sin_v, in_=sin.rearrange("(p t) d -> p t d", t=T_PER_PART))
+        for i in range(2, N_GROUPS):
+            load_x(i)
+
+        nc.vector.tensor_copy(
+            out=w_grp[:].rearrange("p (c t) -> p c t", t=4),
+            in_=w_raw[:].rearrange("p (t c) -> p c t", t=4),
+        )
+        nc.vector.quantize_mx(
+            out=w_codes[:, 0:QK_COLS].bitcast(FP8X4),
+            scales=w_scales[:, 0:QK_COLS],
+            in_=w_grp[:, 0 : 4 * QK_COLS],
+        )
+        nc.vector.quantize_mx(
+            out=w_codes[:, QK_COLS : QK_COLS + V_COLS].bitcast(FP8X4),
+            scales=w_scales[:, QK_COLS : QK_COLS + V_COLS],
+            in_=w_grp[:, 4 * QK_COLS : 4 * (QK_COLS + V_COLS)],
+        )
+
+        transpose_group(0)
+        copy_group(0)
+        quantise_group(0)
+        transpose_group(1)
+        copy_group(1)
+        quantise_group(1)
+        nc.vector.tensor_scalar_mul(out=sin_v[:, :, 0:HALF], in0=sin_v[:, :, 0:HALF], scalar1=-1.0)
+        project_group(0)
+
+        for i in range(N_GROUPS):
+            if i + 2 < N_GROUPS:
+                transpose_group(i + 2)
+            v_out = copy_v(i)
+            if i + 2 < N_GROUPS:
+                copy_group(i + 2)
+            if i + 1 < N_GROUPS:
+                project_group(i + 1)
+            if i + 1 < N_GROUPS:
+                rope_products(i, 0)
+                rope_products(i, 1)
+                if i + 2 < N_GROUPS:
+                    quantise_group(i + 2)
+                rope_sum(i, nc.gpsimd, 0, TILES)
+            else:
+                rope_products(i, 0)
+                rope_sum(i, nc.gpsimd, 0, 2)
+                rope_products(i, 1)
+                rope_sum(i, nc.vector, 2, TILES)
+            store_group(i, v_out)

@@ -112,76 +112,63 @@ def tile_attention_pa_t_kernel(tc, hidden_states, cos, sin, w_qkv, out_0, out_1,
 
         def project_group(i):
             codes, scales = code_tiles[i]
-            v_ps = ps_v.tile([P, 512], F32, name="v_ps", tag="v_ps")
-            banks = []
-            for pr in range(2):
-                qk_ps = ps_qk.tile([P, 512], F32, name="qk_ps", tag="qk_ps")
-                for j in range(2):
-                    tl = 2 * pr + j
-                    cols = slice(tl * P, (tl + 1) * P)
+            banks = [
+                ps_qk.tile([P, 512], F32, name="q_ps", tag="qk_ps"),
+                ps_qk.tile([P, 512], F32, name="k_ps", tag="qk_ps"),
+                ps_v.tile([P, 512], F32, name="v_ps", tag="v_ps"),
+            ]
+            for tl in range(TILES):
+                cols = slice(tl * P, (tl + 1) * P)
+                for part in range(3):
+                    w_cols = slice(part * P, (part + 1) * P)
                     nc.tensor.matmul_mx(
-                        out=qk_ps[:, j * QK_COLS : (j + 1) * QK_COLS],
+                        out=banks[part][:, cols],
                         lhsT=codes[:, cols].bitcast(FP8X4),
                         lhsT_scale=scales[:, cols],
-                        rhs=w_codes[:, 0:QK_COLS].bitcast(FP8X4),
-                        rhs_scale=w_scales[:, 0:QK_COLS],
+                        rhs=w_codes[:, w_cols].bitcast(FP8X4),
+                        rhs_scale=w_scales[:, w_cols],
                         start=True,
                         stop=True,
                     )
-                    nc.tensor.matmul_mx(
-                        out=v_ps[:, cols],
-                        lhsT=codes[:, cols].bitcast(FP8X4),
-                        lhsT_scale=scales[:, cols],
-                        rhs=w_codes[:, QK_COLS : QK_COLS + V_COLS].bitcast(FP8X4),
-                        rhs_scale=w_scales[:, QK_COLS : QK_COLS + V_COLS],
-                        start=True,
-                        stop=True,
-                    )
-                banks.append(qk_ps)
-            qk_banks[i] = banks
-            v_banks[i] = v_ps
+            qk_banks[i] = banks[:2]
+            v_banks[i] = banks[2]
 
-        def rope_products(i, pr):
-            gg = i % GROUPS_PER_BATCH
-            if pr == 0:
+        def rope_products(i, part, lo=0, hi=TILES):
+            n = hi - lo
+            if i not in prod_tiles:
                 pa = rpool.tile([P, TILES * QK_COLS], F32, name="pa", tag="pa")
                 pb = rpool.tile([P, TILES * QK_COLS], F32, name="pb", tag="pb")
                 prod_tiles[i] = (pa, pb)
             pa, pb = prod_tiles[i]
-            t0 = gg * TILES + 2 * pr
-            bank = qk_banks[i][pr][:].rearrange("p (j h d) -> p j h d", j=2, d=HEAD)
-            pa_v = pa[:].rearrange("p (t h d) -> p t h d", t=TILES, d=HEAD)[:, 2 * pr : 2 * pr + 2, :, :]
-            pb_v = pb[:].rearrange("p (t h d) -> p t h d", t=TILES, d=HEAD)[:, 2 * pr : 2 * pr + 2, :, :]
+            t0 = (i % GROUPS_PER_BATCH) * TILES + lo
+            bank = qk_banks[i][part][:].rearrange("p (t h d) -> p t h d", h=2, d=HEAD)[:, lo:hi, :, :]
+            pa_v = pa[:].rearrange("p (g t h d) -> p g t h d", g=2, h=2, d=HEAD)[:, part, lo:hi, :, :]
+            pb_v = pb[:].rearrange("p (g t h d) -> p g t h d", g=2, h=2, d=HEAD)[:, part, lo:hi, :, :]
             nc.vector.tensor_tensor(
                 out=pa_v,
                 in0=bank,
-                in1=cos_v[:, t0 : t0 + 2, :].unsqueeze(2).to_broadcast([P, 2, 4, HEAD]),
+                in1=cos_v[:, t0 : t0 + n, :].unsqueeze(2).to_broadcast([P, n, 2, HEAD]),
                 op=MULT,
             )
             nc.vector.tensor_tensor(
                 out=pb_v[:, :, :, 0:HALF],
                 in0=bank[:, :, :, HALF:HEAD],
-                in1=sin_v[:, t0 : t0 + 2, 0:HALF].unsqueeze(2).to_broadcast([P, 2, 4, HALF]),
+                in1=sin_v[:, t0 : t0 + n, 0:HALF].unsqueeze(2).to_broadcast([P, n, 2, HALF]),
                 op=MULT,
             )
             nc.vector.tensor_tensor(
                 out=pb_v[:, :, :, HALF:HEAD],
                 in0=bank[:, :, :, 0:HALF],
-                in1=sin_v[:, t0 : t0 + 2, HALF:HEAD].unsqueeze(2).to_broadcast([P, 2, 4, HALF]),
+                in1=sin_v[:, t0 : t0 + n, HALF:HEAD].unsqueeze(2).to_broadcast([P, n, 2, HALF]),
                 op=MULT,
             )
 
-        def rope_sum(i, engine, t_lo, t_hi):
+        def rope_sum(i, engine, lo, hi):
             pa, pb = prod_tiles[i]
             if i not in out_tiles:
-                qk_out = opool.tile([P, 2 * TILES * P], F32, name="qk_out", tag="qk_out")
-                out_tiles[i] = qk_out
-            qk_out = out_tiles[i]
+                out_tiles[i] = opool.tile([P, 2 * TILES * P], F32, name="qk_out", tag="qk_out")
             engine.tensor_tensor(
-                out=qk_out[:].rearrange("p (g t c) -> p t g c", g=2, c=P)[:, t_lo:t_hi, :, :],
-                in0=pa[:].rearrange("p (t g c) -> p t g c", g=2, c=P)[:, t_lo:t_hi, :, :],
-                in1=pb[:].rearrange("p (t g c) -> p t g c", g=2, c=P)[:, t_lo:t_hi, :, :],
-                op=ADD,
+                out=out_tiles[i][:, lo:hi], in0=pa[:, lo:hi], in1=pb[:, lo:hi], op=ADD
             )
 
         def copy_v(i):
@@ -250,10 +237,10 @@ def tile_attention_pa_t_kernel(tc, hidden_states, cos, sin, w_qkv, out_0, out_1,
                 rope_products(i, 1)
                 if i + 2 < N_GROUPS:
                     quantise_group(i + 2)
-                rope_sum(i, nc.gpsimd, 0, TILES)
+                rope_sum(i, nc.gpsimd, 0, 1024)
             else:
                 rope_products(i, 0)
-                rope_sum(i, nc.gpsimd, 0, 2)
+                rope_sum(i, nc.gpsimd, 0, 512)
                 rope_products(i, 1)
-                rope_sum(i, nc.vector, 2, TILES)
+                rope_sum(i, nc.vector, 512, 1024)
             store_group(i, v_out)

@@ -23,6 +23,7 @@ T_PER_PART = SEQ // P
 TILES = 4
 GROUPS_PER_BATCH = T_PER_PART // TILES
 N_GROUPS = BATCH * GROUPS_PER_BATCH
+PE_SUM = 128
 
 FLOPS = 2 * BATCH * SEQ * HID * (QK_COLS + V_COLS)
 
@@ -43,7 +44,8 @@ def tile_attention_pa_t_kernel(tc, hidden_states, cos, sin, w_qkv, out_0, out_1,
         opool = ctx.enter_context(tc.tile_pool(name="opool", bufs=N_GROUPS))
         ps_x = ctx.enter_context(tc.psum_pool(name="ps_x", bufs=2))
         ps_qk = ctx.enter_context(tc.psum_pool(name="ps_qk", bufs=4))
-        ps_v = ctx.enter_context(tc.psum_pool(name="ps_v", bufs=2))
+        ps_v = ctx.enter_context(tc.psum_pool(name="ps_v", bufs=1))
+        ps_s = ctx.enter_context(tc.psum_pool(name="ps_s", bufs=1))
         ctx.enter_context(tc.manual_schedule())
 
         x_tiles = {}
@@ -54,6 +56,8 @@ def tile_attention_pa_t_kernel(tc, hidden_states, cos, sin, w_qkv, out_0, out_1,
         v_banks = {}
         prod_tiles = {}
         out_tiles = {}
+        sum_banks = {}
+        v_outs = {}
 
         ident = const.tile([P, P], F32, name="ident")
         make_identity(nc, ident[:])
@@ -163,6 +167,17 @@ def tile_attention_pa_t_kernel(tc, hidden_states, cos, sin, w_qkv, out_0, out_1,
                 op=MULT,
             )
 
+        def pe_sum(i):
+            pa, pb = prod_tiles[i]
+            s_ps = ps_s.tile([P, PE_SUM], F32, name="s_ps", tag="s_ps")
+            cols = slice(1024 - PE_SUM, 1024)
+            nc.tensor.matmul(out=s_ps[:], lhsT=ident[:], rhs=pa[:, cols], start=True, stop=False)
+            nc.tensor.matmul(out=s_ps[:], lhsT=ident[:], rhs=pb[:, cols], start=False, stop=True)
+            sum_banks[i] = s_ps
+
+        def copy_sum(i):
+            nc.scalar.copy(out=out_tiles[i][:, 1024 - PE_SUM : 1024], in_=sum_banks[i][:])
+
         def rope_sum(i, engine, lo, hi):
             pa, pb = prod_tiles[i]
             if i not in out_tiles:
@@ -228,19 +243,25 @@ def tile_attention_pa_t_kernel(tc, hidden_states, cos, sin, w_qkv, out_0, out_1,
             if i + 2 < N_GROUPS:
                 transpose_group(i + 2)
             v_out = copy_v(i)
+            if i > 0:
+                pe_sum(i - 1)
             if i + 2 < N_GROUPS:
                 copy_group(i + 2)
             if i + 1 < N_GROUPS:
                 project_group(i + 1)
+            if i > 0:
+                copy_sum(i - 1)
+                store_group(i - 1, v_outs[i - 1])
+            v_outs[i] = v_out
             if i + 1 < N_GROUPS:
                 rope_products(i, 0)
                 rope_products(i, 1)
                 if i + 2 < N_GROUPS:
                     quantise_group(i + 2)
-                rope_sum(i, nc.gpsimd, 0, 1024)
+                rope_sum(i, nc.gpsimd, 0, 1024 - PE_SUM)
             else:
                 rope_products(i, 0)
                 rope_sum(i, nc.gpsimd, 0, 512)
                 rope_products(i, 1)
                 rope_sum(i, nc.vector, 512, 1024)
-            store_group(i, v_out)
+                store_group(i, v_out)

@@ -23,7 +23,7 @@ T_PER_PART = SEQ // P
 TILES = 4
 GROUPS_PER_BATCH = T_PER_PART // TILES
 N_GROUPS = BATCH * GROUPS_PER_BATCH
-PE_SUM = 128
+PE_SUM = 96
 
 FLOPS = 2 * BATCH * SEQ * HID * (QK_COLS + V_COLS)
 
@@ -167,23 +167,26 @@ def tile_attention_pa_t_kernel(tc, hidden_states, cos, sin, w_qkv, out_0, out_1,
                 op=MULT,
             )
 
-        def pe_sum(i):
+        def pe_sum(i, lo, hi):
             pa, pb = prod_tiles[i]
-            s_ps = ps_s.tile([P, PE_SUM], F32, name="s_ps", tag="s_ps")
-            cols = slice(1024 - PE_SUM, 1024)
-            nc.tensor.matmul(out=s_ps[:], lhsT=ident[:], rhs=pa[:, cols], start=True, stop=False)
-            nc.tensor.matmul(out=s_ps[:], lhsT=ident[:], rhs=pb[:, cols], start=False, stop=True)
-            sum_banks[i] = s_ps
+            s_ps = ps_s.tile([P, 2 * PE_SUM], F32, name="s_ps", tag="s_ps")
+            out = s_ps[:, 0 : hi - lo]
+            nc.tensor.matmul(out=out, lhsT=ident[:], rhs=pa[:, lo:hi], start=True, stop=False)
+            nc.tensor.matmul(out=out, lhsT=ident[:], rhs=pb[:, lo:hi], start=False, stop=True)
+            sum_banks[i] = out
 
-        def copy_sum(i):
-            nc.scalar.copy(out=out_tiles[i][:, 1024 - PE_SUM : 1024], in_=sum_banks[i][:])
+        def copy_sum(i, lo, hi):
+            nc.scalar.copy(out=out_sb(i)[:, lo:hi], in_=sum_banks[i])
+
+        def out_sb(i):
+            if i not in out_tiles:
+                out_tiles[i] = opool.tile([P, 2 * TILES * P], F32, name="qk_out", tag="qk_out")
+            return out_tiles[i]
 
         def rope_sum(i, engine, lo, hi):
             pa, pb = prod_tiles[i]
-            if i not in out_tiles:
-                out_tiles[i] = opool.tile([P, 2 * TILES * P], F32, name="qk_out", tag="qk_out")
             engine.tensor_tensor(
-                out=out_tiles[i][:, lo:hi], in0=pa[:, lo:hi], in1=pb[:, lo:hi], op=ADD
+                out=out_sb(i)[:, lo:hi], in0=pa[:, lo:hi], in1=pb[:, lo:hi], op=ADD
             )
 
         def copy_v(i):
@@ -191,18 +194,21 @@ def tile_attention_pa_t_kernel(tc, hidden_states, cos, sin, w_qkv, out_0, out_1,
             nc.scalar.copy(out=v_out[:], in_=v_banks[i][:])
             return v_out
 
-        def store_group(i, v_out):
+        def store(rows, sb, i):
             b, gg = divmod(i, GROUPS_PER_BATCH)
-            ts = slice(gg * TILES, (gg + 1) * TILES)
-            qk_out = out_tiles[i]
-            nc.sync.dma_start(out=vv[b, :, ts, :], in_=v_out[:].rearrange("p (t c) -> p t c", c=P))
             nc.sync.dma_start(
-                out=qv[b, :, ts, :], in_=qk_out[:, 0 : TILES * P].rearrange("p (t c) -> p t c", c=P)
+                out=rows[b, :, gg * TILES : (gg + 1) * TILES, :],
+                in_=sb.rearrange("p (t c) -> p t c", c=P),
             )
-            nc.sync.dma_start(
-                out=kv[b, :, ts, :],
-                in_=qk_out[:, TILES * P : 2 * TILES * P].rearrange("p (t c) -> p t c", c=P),
-            )
+
+        def store_v(i):
+            store(vv, v_outs[i][:], i)
+
+        def store_q(i):
+            store(qv, out_tiles[i][:, 0:512], i)
+
+        def store_k(i):
+            store(kv, out_tiles[i][:, 512:1024], i)
 
         load_x(0)
         nc.sync.dma_start(
@@ -239,29 +245,43 @@ def tile_attention_pa_t_kernel(tc, hidden_states, cos, sin, w_qkv, out_0, out_1,
         nc.vector.tensor_scalar_mul(out=sin_v[:, :, 0:HALF], in0=sin_v[:, :, 0:HALF], scalar1=-1.0)
         project_group(0)
 
-        for i in range(N_GROUPS):
-            if i + 2 < N_GROUPS:
+        last = N_GROUPS - 1
+        for i in range(last):
+            if i + 2 <= last:
                 transpose_group(i + 2)
-            v_out = copy_v(i)
+            v_outs[i] = copy_v(i)
             if i > 0:
-                pe_sum(i - 1)
-            if i + 2 < N_GROUPS:
+                pe_sum(i - 1, 1024 - PE_SUM, 1024)
+            if i + 2 <= last:
                 copy_group(i + 2)
-            if i + 1 < N_GROUPS:
-                project_group(i + 1)
+            project_group(i + 1)
             if i > 0:
-                copy_sum(i - 1)
-                store_group(i - 1, v_outs[i - 1])
-            v_outs[i] = v_out
-            if i + 1 < N_GROUPS:
-                rope_products(i, 0)
-                rope_products(i, 1)
-                if i + 2 < N_GROUPS:
-                    quantise_group(i + 2)
+                copy_sum(i - 1, 1024 - PE_SUM, 1024)
+                store_v(i - 1)
+                store_q(i - 1)
+                store_k(i - 1)
+            rope_products(i, 0)
+            rope_products(i, 1)
+            if i + 2 <= last:
+                quantise_group(i + 2)
+            if i < last - 1:
                 rope_sum(i, nc.gpsimd, 0, 1024 - PE_SUM)
-            else:
-                rope_products(i, 0)
-                rope_sum(i, nc.gpsimd, 0, 512)
-                rope_products(i, 1)
-                rope_sum(i, nc.vector, 512, 1024)
-                store_group(i, v_out)
+
+        i = last - 1
+        rope_sum(i, nc.gpsimd, 0, 512)
+        rope_sum(i, nc.gpsimd, 512, 1024 - 2 * PE_SUM)
+        pe_sum(i, 1024 - 2 * PE_SUM, 1024)
+        store_v(i)
+        v_outs[last] = copy_v(last)
+        store_v(last)
+        copy_sum(i, 1024 - 2 * PE_SUM, 1024)
+        store_q(i)
+        store_k(i)
+        rope_products(last, 0)
+        pe_sum(last, 512 - 2 * PE_SUM, 512)
+        copy_sum(last, 512 - 2 * PE_SUM, 512)
+        rope_products(last, 1)
+        rope_sum(last, nc.vector, 512, 1024)
+        store_k(last)
+        rope_sum(last, nc.vector, 0, 512 - 2 * PE_SUM)
+        store_q(last)

@@ -137,33 +137,28 @@ def tile_attention_pa_t_kernel(tc, hidden_states, cos, sin, w_qkv, out_0, out_1,
             qk_banks[i] = banks[:2]
             v_banks[i] = banks[2]
 
-        def rope_products(i, part, lo=0, hi=TILES):
-            n = hi - lo
+        def rope_products(i, part):
             if i not in prod_tiles:
                 pa = rpool.tile([P, TILES * QK_COLS], F32, name="pa", tag="pa")
                 pb = rpool.tile([P, TILES * QK_COLS], F32, name="pb", tag="pb")
                 prod_tiles[i] = (pa, pb)
             pa, pb = prod_tiles[i]
-            t0 = (i % GROUPS_PER_BATCH) * TILES + lo
-            bank = qk_banks[i][part][:].rearrange("p (t h d) -> p t h d", h=2, d=HEAD)[:, lo:hi, :, :]
-            pa_v = pa[:].rearrange("p (g t h d) -> p g t h d", g=2, h=2, d=HEAD)[:, part, lo:hi, :, :]
-            pb_v = pb[:].rearrange("p (g t h d) -> p g t h d", g=2, h=2, d=HEAD)[:, part, lo:hi, :, :]
+            t0 = (i % GROUPS_PER_BATCH) * TILES
+            bank = qk_banks[i][part][:]
+            cols = slice(part * 512, (part + 1) * 512)
             nc.vector.tensor_tensor(
-                out=pa_v,
-                in0=bank,
-                in1=cos_v[:, t0 : t0 + n, :].unsqueeze(2).to_broadcast([P, n, 2, HEAD]),
+                out=pa[:, cols].rearrange("p (t h d) -> p t h d", h=2, d=HEAD),
+                in0=bank.rearrange("p (t h d) -> p t h d", h=2, d=HEAD),
+                in1=cos_v[:, t0 : t0 + TILES, :].unsqueeze(2).to_broadcast([P, TILES, 2, HEAD]),
                 op=MULT,
             )
             nc.vector.tensor_tensor(
-                out=pb_v[:, :, :, 0:HALF],
-                in0=bank[:, :, :, HALF:HEAD],
-                in1=sin_v[:, t0 : t0 + n, 0:HALF].unsqueeze(2).to_broadcast([P, n, 2, HALF]),
-                op=MULT,
-            )
-            nc.vector.tensor_tensor(
-                out=pb_v[:, :, :, HALF:HEAD],
-                in0=bank[:, :, :, 0:HALF],
-                in1=sin_v[:, t0 : t0 + n, HALF:HEAD].unsqueeze(2).to_broadcast([P, n, 2, HALF]),
+                out=pb[:, cols].rearrange("p (t h s d) -> p t h s d", h=2, s=2, d=HALF),
+                in0=bank.rearrange("p (t h s d) -> p t h s d", h=2, s=2, d=HALF)[:, :, :, ::-1, :],
+                in1=sin_v[:, t0 : t0 + TILES, :]
+                .rearrange("p t (s d) -> p t s d", d=HALF)
+                .unsqueeze(2)
+                .to_broadcast([P, TILES, 2, 2, HALF]),
                 op=MULT,
             )
 

from contextlib import ExitStack

import concourse.mybir as mybir
from concourse.masks import make_identity

F32 = mybir.dt.float32
BF16 = mybir.dt.bfloat16
U32 = mybir.dt.uint32
U8 = mybir.dt.uint8
FP8X4 = mybir.dt.float8_e4m3fn_x4
MULT = mybir.AluOpType.mult
ADD = mybir.AluOpType.add

P = 128
BATCH = 4
SEQ = 2048
HID = 512
HEAD = 64
HALF = 32
QK_COLS = 256
V_COLS = 128
T_PER_PART = SEQ // P
TILES = 4
GROUPS_PER_BATCH = T_PER_PART // TILES
N_GROUPS = BATCH * GROUPS_PER_BATCH
PE_SUM = 96

FLOPS = 2 * BATCH * SEQ * HID * (QK_COLS + V_COLS)


def tile_attention_pa_t_kernel(tc, hidden_states, cos, sin, w_qkv, out_0, out_1, out_2):
    nc = tc.nc
    xv = hidden_states.rearrange("b (p t) k -> b p t k", t=T_PER_PART)
    qv = out_0.rearrange("b (p t) h d -> b p t (h d)", t=T_PER_PART)
    kv = out_1.rearrange("b (p t) h d -> b p t (h d)", t=T_PER_PART)
    vv = out_2.rearrange("b (p t) h d -> b p t (h d)", t=T_PER_PART)

    with ExitStack() as ctx:
        const = ctx.enter_context(tc.tile_pool(name="const", bufs=1))
        xpool = ctx.enter_context(tc.tile_pool(name="xpool", bufs=N_GROUPS))
        gpool = ctx.enter_context(tc.tile_pool(name="gpool", bufs=3))
        cpool = ctx.enter_context(tc.tile_pool(name="cpool", bufs=3))
        rpool = ctx.enter_context(tc.tile_pool(name="rpool", bufs=3))
        opool = ctx.enter_context(tc.tile_pool(name="opool", bufs=N_GROUPS))
        ps_x = ctx.enter_context(tc.psum_pool(name="ps_x", bufs=2))
        ps_qk = ctx.enter_context(tc.psum_pool(name="ps_qk", bufs=4))
        ps_v = ctx.enter_context(tc.psum_pool(name="ps_v", bufs=1))
        ps_s = ctx.enter_context(tc.psum_pool(name="ps_s", bufs=1))
        ctx.enter_context(tc.manual_schedule())

        x_tiles = {}
        xt_tiles = {}
        grouped_tiles = {}
        code_tiles = {}
        qk_banks = {}
        v_banks = {}
        prod_tiles = {}
        out_tiles = {}
        sum_banks = {}
        v_outs = {}

        ident = const.tile([P, P], F32, name="ident")
        make_identity(nc, ident[:])

        w_raw = const.tile([P, 4 * (QK_COLS + V_COLS)], BF16, name="w_raw")
        w_grp = const.tile([P, 4 * (QK_COLS + V_COLS)], BF16, name="w_grp", align_bytes=64)
        w_codes = const.tile([P, QK_COLS + V_COLS], U32, name="w_codes", align_bytes=64)
        w_scales = const.tile([P, QK_COLS + V_COLS], U8, name="w_scales", align_bytes=64)
        cos_sb = const.tile([P, T_PER_PART * HEAD], BF16, name="cos_sb")
        sin_sb = const.tile([P, T_PER_PART * HEAD], BF16, name="sin_sb")
        cos_v = cos_sb[:].rearrange("p (t d) -> p t d", d=HEAD)
        sin_v = sin_sb[:].rearrange("p (t d) -> p t d", d=HEAD)

        def load_x(i):
            b, gg = divmod(i, GROUPS_PER_BATCH)
            x_sb = xpool.tile([P, TILES * HID], BF16, name="x_sb", tag="x_sb")
            nc.sync.dma_start(
                out=x_sb[:].rearrange("p (t k) -> p t k", k=HID),
                in_=xv[b, :, gg * TILES : (gg + 1) * TILES, :],
            )
            x_tiles[i] = x_sb

        def transpose_group(i):
            words = x_tiles[i][:].bitcast(F32)
            banks = []
            for pr in range(2):
                xt = ps_x.tile([P, 512], F32, name="xt", tag="xt")
                for j in range(2):
                    for u in range(2):
                        base = (2 * pr + j) * 256
                        nc.tensor.transpose(
                            xt[:, u * 256 + j * P : u * 256 + (j + 1) * P],
                            words[:, base + u : base + 256 : 2],
                            ident[:],
                        )
                banks.append(xt)
            xt_tiles[i] = banks

        def copy_group(i):
            grouped = gpool.tile([P, TILES * HID], BF16, name="grouped", tag="grouped", align_bytes=64)
            gw = grouped[:].bitcast(F32)
            for pr in range(2):
                nc.scalar.copy(
                    out=gw[:, pr * 512 : (pr + 1) * 512].rearrange("p (m u) -> p m u", u=2),
                    in_=xt_tiles[i][pr][:].rearrange("p (u m) -> p m u", u=2),
                )
            grouped_tiles[i] = grouped

        def quantise_group(i):
            codes = cpool.tile([P, TILES * P], U32, name="codes", tag="codes", align_bytes=64)
            scales = cpool.tile([P, TILES * P], U8, name="scales", tag="scales", align_bytes=64)
            nc.vector.quantize_mx(
                out=codes[:].bitcast(FP8X4), scales=scales[:], in_=grouped_tiles[i][:]
            )
            code_tiles[i] = (codes, scales)

        def project_group(i):
            codes, scales = code_tiles[i]
            banks = [
                ps_qk.tile([P, 512], F32, name="q_ps", tag="qk_ps"),
                ps_qk.tile([P, 512], F32, name="k_ps", tag="qk_ps"),
                ps_v.tile([P, 512], F32, name="v_ps", tag="v_ps"),
            ]
            for tl in range(TILES):
                cols = slice(tl * P, (tl + 1) * P)
                for part in range(3):
                    w_cols = slice(part * P, (part + 1) * P)
                    nc.tensor.matmul_mx(
                        out=banks[part][:, cols],
                        lhsT=codes[:, cols].bitcast(FP8X4),
                        lhsT_scale=scales[:, cols],
                        rhs=w_codes[:, w_cols].bitcast(FP8X4),
                        rhs_scale=w_scales[:, w_cols],
                        start=True,
                        stop=True,
                    )
            qk_banks[i] = banks[:2]
            v_banks[i] = banks[2]

        def rope_products(i, part):
            if i not in prod_tiles:
                pa = rpool.tile([P, TILES * QK_COLS], F32, name="pa", tag="pa")
                pb = rpool.tile([P, TILES * QK_COLS], F32, name="pb", tag="pb")
                prod_tiles[i] = (pa, pb)
            pa, pb = prod_tiles[i]
            t0 = (i % GROUPS_PER_BATCH) * TILES
            bank = qk_banks[i][part][:]
            cols = slice(part * 512, (part + 1) * 512)
            nc.vector.tensor_tensor(
                out=pa[:, cols].rearrange("p (t h d) -> p t h d", h=2, d=HEAD),
                in0=bank.rearrange("p (t h d) -> p t h d", h=2, d=HEAD),
                in1=cos_v[:, t0 : t0 + TILES, :].unsqueeze(2).to_broadcast([P, TILES, 2, HEAD]),
                op=MULT,
            )
            nc.vector.tensor_tensor(
                out=pb[:, cols].rearrange("p (t h s d) -> p t h s d", h=2, s=2, d=HALF),
                in0=bank.rearrange("p (t h s d) -> p t h s d", h=2, s=2, d=HALF)[:, :, :, ::-1, :],
                in1=sin_v[:, t0 : t0 + TILES, :]
                .rearrange("p t (s d) -> p t s d", d=HALF)
                .unsqueeze(2)
                .to_broadcast([P, TILES, 2, 2, HALF]),
                op=MULT,
            )

        def pe_sum(i, lo, hi):
            pa, pb = prod_tiles[i]
            s_ps = ps_s.tile([P, 2 * PE_SUM], F32, name="s_ps", tag="s_ps")
            out = s_ps[:, 0 : hi - lo]
            nc.tensor.matmul(out=out, lhsT=ident[:], rhs=pa[:, lo:hi], start=True, stop=False)
            nc.tensor.matmul(out=out, lhsT=ident[:], rhs=pb[:, lo:hi], start=False, stop=True)
            sum_banks[i] = out

        def copy_sum(i, lo, hi):
            nc.scalar.copy(out=out_sb(i)[:, lo:hi], in_=sum_banks[i])

        def out_sb(i):
            if i not in out_tiles:
                out_tiles[i] = opool.tile([P, 2 * TILES * P], F32, name="qk_out", tag="qk_out")
            return out_tiles[i]

        def rope_sum(i, engine, lo, hi):
            pa, pb = prod_tiles[i]
            engine.tensor_tensor(
                out=out_sb(i)[:, lo:hi], in0=pa[:, lo:hi], in1=pb[:, lo:hi], op=ADD
            )

        def copy_v(i):
            v_out = opool.tile([P, TILES * P], F32, name="v_out", tag="v_out")
            nc.scalar.copy(out=v_out[:], in_=v_banks[i][:])
            return v_out

        def store(rows, sb, i):
            b, gg = divmod(i, GROUPS_PER_BATCH)
            nc.sync.dma_start(
                out=rows[b, :, gg * TILES : (gg + 1) * TILES, :],
                in_=sb.rearrange("p (t c) -> p t c", c=P),
            )

        def store_v(i):
            store(vv, v_outs[i][:], i)

        def store_q(i):
            store(qv, out_tiles[i][:, 0:512], i)

        def store_k(i):
            store(kv, out_tiles[i][:, 512:1024], i)

        load_x(0)
        nc.sync.dma_start(
            out=w_raw[:],
            in_=w_qkv.rearrange("(q t) c -> q (t c)", t=4),
        )
        load_x(1)
        nc.sync.dma_start(out=cos_v, in_=cos.rearrange("(p t) d -> p t d", t=T_PER_PART))
        nc.sync.dma_start(out=sin_v, in_=sin.rearrange("(p t) d -> p t d", t=T_PER_PART))
        for i in range(2, N_GROUPS):
            load_x(i)

        nc.vector.tensor_copy(
            out=w_grp[:].rearrange("p (c t) -> p c t", t=4),
            in_=w_raw[:].rearrange("p (t c) -> p c t", t=4),
        )
        nc.vector.quantize_mx(
            out=w_codes[:, 0:QK_COLS].bitcast(FP8X4),
            scales=w_scales[:, 0:QK_COLS],
            in_=w_grp[:, 0 : 4 * QK_COLS],
        )
        nc.vector.quantize_mx(
            out=w_codes[:, QK_COLS : QK_COLS + V_COLS].bitcast(FP8X4),
            scales=w_scales[:, QK_COLS : QK_COLS + V_COLS],
            in_=w_grp[:, 4 * QK_COLS : 4 * (QK_COLS + V_COLS)],
        )

        transpose_group(0)
        copy_group(0)
        quantise_group(0)
        transpose_group(1)
        copy_group(1)
        quantise_group(1)
        nc.vector.tensor_scalar_mul(out=sin_v[:, :, 0:HALF], in0=sin_v[:, :, 0:HALF], scalar1=-1.0)
        project_group(0)

        last = N_GROUPS - 1
        for i in range(last):
            if i + 2 <= last:
                transpose_group(i + 2)
            v_outs[i] = copy_v(i)
            if i > 0:
                pe_sum(i - 1, 1024 - PE_SUM, 1024)
            if i + 2 <= last:
                copy_group(i + 2)
            project_group(i + 1)
            if i > 0:
                copy_sum(i - 1, 1024 - PE_SUM, 1024)
                store_v(i - 1)
                store_q(i - 1)
                store_k(i - 1)
            rope_products(i, 0)
            rope_products(i, 1)
            if i + 2 <= last:
                quantise_group(i + 2)
            if i < last - 1:
                rope_sum(i, nc.gpsimd, 0, 1024 - PE_SUM)

        i = last - 1
        rope_sum(i, nc.gpsimd, 0, 512)
        rope_sum(i, nc.gpsimd, 512, 1024 - 2 * PE_SUM)
        pe_sum(i, 1024 - 2 * PE_SUM, 1024)
        store_v(i)
        v_outs[last] = copy_v(last)
        store_v(last)
        copy_sum(i, 1024 - 2 * PE_SUM, 1024)
        store_q(i)
        store_k(i)
        rope_products(last, 0)
        pe_sum(last, 512 - 2 * PE_SUM, 512)
        copy_sum(last, 512 - 2 * PE_SUM, 512)
        rope_products(last, 1)
        rope_sum(last, nc.vector, 512, 1024)
        store_k(last)
        rope_sum(last, nc.vector, 0, 512 - 2 * PE_SUM)
        store_q(last)
